import numpy as np
import ml_dtypes


BF16 = ml_dtypes.bfloat16


def bf(x):
    return np.asarray(x, np.float32).astype(BF16)


def f64(x):
    return np.asarray(x).astype(np.float64)


E2M1 = np.array([0.0, 0.5, 1.0, 1.5, 2.0, 3.0, 4.0, 6.0, -0.0, -0.5, -1.0, -1.5, -2.0, -3.0, -4.0, -6.0])


def pack_weight(w, fmt):
    k, n = w.shape
    w = f64(bf(w)).reshape(k // 32, 32, n)
    amax = np.abs(w).max(1)
    if fmt == "e4m3":
        byte = np.frexp(amax)[1] - 1 + 127 - 7
    else:
        mant, ex = np.frexp(amax / 6.0)
        byte = np.where(mant > 0.5, ex, ex - 1) + 127
    byte = np.clip(np.where(amax > 0, byte, 1), 1, 254)
    scaled = (w * np.exp2(127.0 - byte)[:, None, :]).reshape(k, n).astype(np.float32)
    by_word = np.ascontiguousarray(scaled.reshape(k // 512, 128, 4, n).transpose(0, 1, 3, 2))
    if fmt == "e4m3":
        words = by_word.astype(ml_dtypes.float8_e4m3fn).view(np.uint8)
    else:
        c = by_word.astype(ml_dtypes.float4_e2m1fn).view(np.uint8) & 0xF
        words = c[..., 0::2] | (c[..., 1::2] << 4)
    return np.ascontiguousarray(words), np.ascontiguousarray(byte.astype(np.uint8).reshape(k // 512, 16, n))


def unpack_weight(words, scales, fmt):
    g, p, n, _ = words.shape
    if fmt == "e4m3":
        vals = np.ascontiguousarray(words).view(ml_dtypes.float8_e4m3fn).astype(np.float64)
    else:
        nib = np.empty((g, p, n, 4), np.uint8)
        nib[..., 0::2] = words & 0xF
        nib[..., 1::2] = words >> 4
        vals = E2M1[nib]
    vals = vals * np.repeat(np.exp2(scales.astype(np.float64) - 127.0), 8, axis=1)[..., None]
    return vals.transpose(0, 1, 3, 2).reshape(g * 512, n)

def pack4(w):
    words, scales = pack_weight(w, "e2m1")
    return words.reshape(words.shape[0], 128, -1), scales


def unpack4(words, scales):
    return unpack_weight(words.reshape(words.shape[0], 128, -1, 2), scales, "e2m1")


def kspread(k):
    return np.exp2(np.repeat(np.random.randint(-6, 7, k // 32), 32).astype(np.float64))


B, T, C, H, W = 1, 128, 3072, 8, 512
D = C // H
HALF = D // 2
ROPE_BASE = 10000.0


def rotate_half(u):
    return np.concatenate([-u[..., HALF:], u[..., :HALF]], axis=-1)


def setup_inputs():
    s = kspread(C)
    start = np.random.randint(0, T)
    inv_freq = 1.0 / (ROPE_BASE ** (np.arange(0, D, 2) / D))
    freqs = np.outer(start + np.arange(T), inv_freq)
    emb = np.concatenate([freqs, freqs], axis=-1)
    x = np.random.standard_normal((B, T, C)) * s
    x_words, x_scales = pack4(np.ascontiguousarray(x.reshape(B * T, C).T))
    words, scales = pack4(np.random.standard_normal((C, 3 * C)) * 1.25 / np.sqrt(C) / s[:, None])
    return {"x_words": x_words,
            "x_scales": x_scales,
            "freqs_cos": bf(np.cos(emb)),
            "freqs_sin": bf(np.sin(emb)),
            "w_attn_words": words,
            "w_attn_scales": scales}


def reference(x_words, x_scales, freqs_cos, freqs_sin, w_attn_words, w_attn_scales):
    qkv = unpack4(x_words, x_scales).T.reshape(B, T, C) @ unpack4(w_attn_words, w_attn_scales)
    q, k, v = np.split(qkv, 3, axis=-1)
    q = q.reshape(B, T, H, D).transpose(0, 2, 1, 3)
    k = k.reshape(B, T, H, D).transpose(0, 2, 1, 3)
    v = v.reshape(B, T, H, D).transpose(0, 2, 1, 3)
    cos = f64(freqs_cos)[None, None, :, :]
    sin = f64(freqs_sin)[None, None, :, :]
    q_rot = q * cos + rotate_half(q) * sin
    k_rot = k * cos + rotate_half(k) * sin
    return q_rot, k_rot, v

@@ -1,0 +1,164 @@
+from contextlib import ExitStack
+
+import concourse.mybir as mybir
+
+FLOPS = 2 * 128 * 3072 * 9216
+
+F32 = mybir.dt.float32
+BF16 = mybir.dt.bfloat16
+I32 = mybir.dt.int32
+U8 = mybir.dt.uint8
+FP4X4 = mybir.dt.float4_e2m1fn_x4
+MULT = mybir.AluOpType.mult
+ADD = mybir.AluOpType.add
+SUB = mybir.AluOpType.subtract
+
+P = 128
+PASSES = 6
+HEAD = 384
+HALF = 192
+TILE = 512
+BANKS = 8
+CHUNK = 2048
+ROPE_COLS = 6144
+COLS = 9216
+
+CHUNKS = [
+    (4, ((0, 1), (2, 3), (4, 5))),
+    (4, ((0, 1), (2, 3), (4, 5))),
+    (4, ((0, 1), (2, 3), (4, 5))),
+    (4, ((0, 1), (2, 3), (4, 5))),
+    (2, ((0, 1, 2, 3), (4,), (5,))),
+]
+
+
+def tile_swaattention_pa_kernel(
+    tc, x_words, x_scales, freqs_cos, freqs_sin, w_attn_words, w_attn_scales, out_0, out_1, out_2
+):
+    nc = tc.nc
+
+    with ExitStack() as ctx:
+        ctx.enter_context(tc.manual_schedule())
+        keep = ctx.enter_context(tc.tile_pool(name="keep", bufs=1))
+        psum = ctx.enter_context(tc.psum_pool(name="psum", bufs=1))
+
+        xw = keep.tile([P, PASSES, 256], U8, name="xw", align_bytes=64)
+        xs = keep.tile([P, PASSES, 128], U8, name="xs", align_bytes=64)
+        planes = [keep.tile([P, COLS], U8, name="plane%d" % g, align_bytes=64) for g in range(PASSES)]
+        cos2 = keep.tile([P, 2 * HEAD], BF16, name="cos2")
+        sin2 = keep.tile([P, 2 * HEAD], BF16, name="sin2")
+        warm = keep.tile([P, 8], F32, name="warm")
+        warm2 = keep.tile([P, 8], F32, name="warm2")
+        t1 = keep.tile([P, ROPE_COLS], F32, name="t1")
+        u = keep.tile([P, ROPE_COLS], F32, name="u")
+        vo = keep.tile([P, 8 * HEAD], F32, name="vo")
+
+        nc.vector.memset(xs[:].bitcast(I32), 0)
+        nc.vector.memset(warm[:], 0.0)
+        for plane in planes:
+            nc.vector.memset(plane[:].bitcast(I32), 0)
+        nc.scalar.copy(out=warm2[:], in_=warm[:])
+
+        for rep in range(2):
+            nc.gpsimd.dma_start(out=cos2[:, rep * HEAD : (rep + 1) * HEAD], in_=freqs_cos[:, :])
+        for rep in range(2):
+            nc.gpsimd.dma_start(out=sin2[:, rep * HEAD : rep * HEAD + HALF], in_=freqs_sin[:, HALF:HEAD])
+            nc.gpsimd.dma_start(out=sin2[:, rep * HEAD + HALF : (rep + 1) * HEAD], in_=freqs_sin[:, 0:HALF])
+
+        code_tiles = {}
+        code_loads = []
+        for c, (nt, groups) in enumerate(CHUNKS):
+            for gi, grp in enumerate(groups):
+                t = keep.tile([P, len(grp), 2 * nt * TILE], U8, name="w%d_%d" % (c, gi), align_bytes=64)
+                code_tiles[(c, gi)] = t
+                code_loads.append((t, grp[0], len(grp), c * CHUNK, nt * TILE))
+
+        def load_codes(item):
+            t, g0, ng, col0, ncols = item
+            nc.sync.dma_start(
+                out=t[:].bitcast(I32),
+                in_=w_attn_words[g0 : g0 + ng, :, 2 * col0 : 2 * (col0 + ncols)]
+                .rearrange("g p n -> p g n")
+                .bitcast(I32),
+            )
+
+        def load_plane(g, r):
+            nc.sync.dma_start(out=planes[g][r:P:32, :].bitcast(I32), in_=w_attn_scales[g, r:16:4, :].bitcast(I32))
+
+        def load_x_scales():
+            for q in range(4):
+                nc.sync.dma_start(
+                    out=xs[32 * q : 32 * q + 4, :, :].bitcast(I32),
+                    in_=x_scales[:, 4 * q : 4 * q + 4, :].rearrange("g r n -> r g n").bitcast(I32),
+                )
+
+        nc.sync.dma_start(out=xw[:].bitcast(I32), in_=x_words.rearrange("g p n -> p g n").bitcast(I32))
+        load_codes(code_loads[0])
+        for r in range(4):
+            for g in range(PASSES):
+                load_plane(g, r)
+                if r == 0 and g == 1:
+                    load_codes(code_loads[1])
+            if r == 0:
+                load_x_scales()
+        for item in code_loads[2:]:
+            load_codes(item)
+
+        def store(queue, out, a, b, src, h_lo):
+            queue.dma_start(
+                out=out[0, a:b].rearrange("h p d -> p h d"),
+                in_=src[:, h_lo * HEAD : (h_lo + b - a) * HEAD].rearrange("p (h d) -> p h d", d=HEAD),
+            )
+
+        for c, (nt, groups) in enumerate(CHUNKS):
+            accs = []
+            for j in range(nt):
+                accs.append(
+                    psum.tile([P, TILE], F32, name="acc%d_%d" % (c, j), tag="bank%d" % ((4 * c + j) % BANKS))
+                )
+            for gi, grp in enumerate(groups):
+                t = code_tiles[(c, gi)]
+                for k, g in enumerate(grp):
+                    for j in range(nt):
+                        nc.tensor.matmul_mx(
+                            out=accs[j][:],
+                            lhsT=xw[:, g, :].bitcast(FP4X4),
+                            lhsT_scale=xs[:, g, :],
+                            rhs=t[:, k, 2 * j * TILE : 2 * (j + 1) * TILE].bitcast(FP4X4),
+                            rhs_scale=planes[g][:, c * CHUNK + j * TILE : c * CHUNK + (j + 1) * TILE],
+                            start=(g == 0),
+                            stop=(g == PASSES - 1),
+                        )
+
+            col0 = c * CHUNK
+            col1 = col0 + nt * TILE
+            if col0 < ROPE_COLS:
+                for j in range(nt):
+                    off = col0 + j * TILE
+                    toff = off % HEAD
+                    nc.vector.tensor_tensor(
+                        out=t1[:, off : off + TILE], in0=accs[j][:], in1=cos2[:, toff : toff + TILE], op=MULT
+                    )
+                    nc.vector.tensor_tensor(
+                        out=u[:, off : off + TILE], in0=accs[j][:], in1=sin2[:, toff : toff + TILE], op=MULT
+                    )
+                h_lo = col0 // HEAD
+                h_hi = col1 // HEAD
+                rv = t1[:, h_lo * HEAD : h_hi * HEAD].rearrange("p (h s d) -> p h s d", s=2, d=HALF)
+                uv = u[:, h_lo * HEAD : h_hi * HEAD].rearrange("p (h s d) -> p h s d", s=2, d=HALF)
+                nc.vector.tensor_tensor(out=rv[:, :, 0, :], in0=rv[:, :, 0, :], in1=uv[:, :, 1, :], op=SUB)
+                nc.vector.tensor_tensor(out=rv[:, :, 1, :], in0=rv[:, :, 1, :], in1=uv[:, :, 0, :], op=ADD)
+                if h_lo < 8:
+                    store(nc.gpsimd, out_0, h_lo, min(h_hi, 8), t1, h_lo)
+                if h_hi > 8:
+                    store(nc.gpsimd, out_1, max(h_lo, 8) - 8, h_hi - 8, t1, max(h_lo, 8))
+            else:
+                for j in range(nt):
+                    off = col0 - ROPE_COLS + j * TILE
+                    if c == len(CHUNKS) - 1 and j == nt - 1:
+                        nc.vector.tensor_copy(out=vo[:, off : off + TILE], in_=accs[j][:])
+                    else:
+                        nc.scalar.copy(out=vo[:, off : off + TILE], in_=accs[j][:])
+                h_lo = (col0 - ROPE_COLS) // HEAD
+                h_hi = (col1 - ROPE_COLS) // HEAD
+                store(nc.sync if c == len(CHUNKS) - 1 else nc.gpsimd, out_2, h_lo, h_hi, vo, h_lo)

@@ -151,14 +151,14 @@ def tile_swaattention_pa_kernel(
                 if h_lo < 8:
                     store(nc.gpsimd, out_0, h_lo, min(h_hi, 8), t1, h_lo)
                 if h_hi > 8:
-                    store(nc.gpsimd, out_1, max(h_lo, 8) - 8, h_hi - 8, t1, max(h_lo, 8))
+                    store(nc.sync if col1 == ROPE_COLS else nc.gpsimd, out_1, max(h_lo, 8) - 8, h_hi - 8, t1, max(h_lo, 8))
             else:
                 for j in range(nt):
                     off = col0 - ROPE_COLS + j * TILE
-                    if c == len(CHUNKS) - 1 and j == nt - 1:
+                    if j % 2 == 1:
                         nc.vector.tensor_copy(out=vo[:, off : off + TILE], in_=accs[j][:])
                     else:
                         nc.scalar.copy(out=vo[:, off : off + TILE], in_=accs[j][:])
                 h_lo = (col0 - ROPE_COLS) // HEAD
                 h_hi = (col1 - ROPE_COLS) // HEAD
-                store(nc.sync if c == len(CHUNKS) - 1 else nc.gpsimd, out_2, h_lo, h_hi, vo, h_lo)
+                store(nc.sync, out_2, h_lo, h_hi, vo, h_lo)

@@ -42,16 +42,16 @@ def tile_swaattention_pa_kernel(
         keep = ctx.enter_context(tc.tile_pool(name="keep", bufs=1))
         psum = ctx.enter_context(tc.psum_pool(name="psum", bufs=1))
 
-        xw = keep.tile([P, PASSES, 256], U8, name="xw", align_bytes=64)
-        xs = keep.tile([P, PASSES, 128], U8, name="xs", align_bytes=64)
-        planes = [keep.tile([P, COLS], U8, name="plane%d" % g, align_bytes=64) for g in range(PASSES)]
+        xw = keep.tile([P, PASSES, 256], U8, name="xw", align_bytes=256)
+        xs = keep.tile([P, PASSES, 128], U8, name="xs", align_bytes=256)
+        planes = [keep.tile([P, COLS], U8, name="plane%d" % g, align_bytes=256) for g in range(PASSES)]
         cos2 = keep.tile([P, 2 * HEAD], BF16, name="cos2")
         sin2 = keep.tile([P, 2 * HEAD], BF16, name="sin2")
         warm = keep.tile([P, 8], F32, name="warm")
         warm2 = keep.tile([P, 8], F32, name="warm2")
-        t1 = keep.tile([P, ROPE_COLS], F32, name="t1")
-        u = keep.tile([P, ROPE_COLS], F32, name="u")
-        vo = keep.tile([P, 8 * HEAD], F32, name="vo")
+        t1 = keep.tile([P, ROPE_COLS], F32, name="t1", align_bytes=256)
+        u = keep.tile([P, ROPE_COLS], F32, name="u", align_bytes=256)
+        vo = keep.tile([P, 8 * HEAD], F32, name="vo", align_bytes=256)
 
         nc.vector.memset(xs[:].bitcast(I32), 0)
         nc.vector.memset(warm[:], 0.0)
@@ -69,7 +69,7 @@ def tile_swaattention_pa_kernel(
         code_loads = []
         for c, (nt, groups) in enumerate(CHUNKS):
             for gi, grp in enumerate(groups):
-                t = keep.tile([P, len(grp), 2 * nt * TILE], U8, name="w%d_%d" % (c, gi), align_bytes=64)
+                t = keep.tile([P, len(grp), 2 * nt * TILE], U8, name="w%d_%d" % (c, gi), align_bytes=256)
                 code_tiles[(c, gi)] = t
                 code_loads.append((t, grp[0], len(grp), c * CHUNK, nt * TILE))
 

from contextlib import ExitStack

import concourse.mybir as mybir

FLOPS = 2 * 128 * 3072 * 9216

F32 = mybir.dt.float32
BF16 = mybir.dt.bfloat16
I32 = mybir.dt.int32
U8 = mybir.dt.uint8
FP4X4 = mybir.dt.float4_e2m1fn_x4
MULT = mybir.AluOpType.mult
ADD = mybir.AluOpType.add
SUB = mybir.AluOpType.subtract

P = 128
PASSES = 6
HEAD = 384
HALF = 192
TILE = 512
BANKS = 8
CHUNK = 2048
ROPE_COLS = 6144
COLS = 9216

CHUNKS = [
    (4, ((0, 1), (2, 3), (4, 5))),
    (4, ((0, 1), (2, 3), (4, 5))),
    (4, ((0, 1), (2, 3), (4, 5))),
    (4, ((0, 1), (2, 3), (4, 5))),
    (2, ((0, 1, 2, 3), (4,), (5,))),
]


def tile_swaattention_pa_kernel(
    tc, x_words, x_scales, freqs_cos, freqs_sin, w_attn_words, w_attn_scales, out_0, out_1, out_2
):
    nc = tc.nc

    with ExitStack() as ctx:
        ctx.enter_context(tc.manual_schedule())
        keep = ctx.enter_context(tc.tile_pool(name="keep", bufs=1))
        psum = ctx.enter_context(tc.psum_pool(name="psum", bufs=1))

        xw = keep.tile([P, PASSES, 256], U8, name="xw", align_bytes=256)
        xs = keep.tile([P, PASSES, 128], U8, name="xs", align_bytes=256)
        planes = [keep.tile([P, COLS], U8, name="plane%d" % g, align_bytes=256) for g in range(PASSES)]
        cos2 = keep.tile([P, 2 * HEAD], BF16, name="cos2")
        sin2 = keep.tile([P, 2 * HEAD], BF16, name="sin2")
        warm = keep.tile([P, 8], F32, name="warm")
        warm2 = keep.tile([P, 8], F32, name="warm2")
        t1 = keep.tile([P, ROPE_COLS], F32, name="t1", align_bytes=256)
        u = keep.tile([P, ROPE_COLS], F32, name="u", align_bytes=256)
        vo = keep.tile([P, 8 * HEAD], F32, name="vo", align_bytes=256)

        nc.vector.memset(xs[:].bitcast(I32), 0)
        nc.vector.memset(warm[:], 0.0)
        for plane in planes:
            nc.vector.memset(plane[:].bitcast(I32), 0)
        nc.scalar.copy(out=warm2[:], in_=warm[:])

        for rep in range(2):
            nc.gpsimd.dma_start(out=cos2[:, rep * HEAD : (rep + 1) * HEAD], in_=freqs_cos[:, :])
        for rep in range(2):
            nc.gpsimd.dma_start(out=sin2[:, rep * HEAD : rep * HEAD + HALF], in_=freqs_sin[:, HALF:HEAD])
            nc.gpsimd.dma_start(out=sin2[:, rep * HEAD + HALF : (rep + 1) * HEAD], in_=freqs_sin[:, 0:HALF])

        code_tiles = {}
        code_loads = []
        for c, (nt, groups) in enumerate(CHUNKS):
            for gi, grp in enumerate(groups):
                t = keep.tile([P, len(grp), 2 * nt * TILE], U8, name="w%d_%d" % (c, gi), align_bytes=256)
                code_tiles[(c, gi)] = t
                code_loads.append((t, grp[0], len(grp), c * CHUNK, nt * TILE))

        def load_codes(item):
            t, g0, ng, col0, ncols = item
            nc.sync.dma_start(
                out=t[:].bitcast(I32),
                in_=w_attn_words[g0 : g0 + ng, :, 2 * col0 : 2 * (col0 + ncols)]
                .rearrange("g p n -> p g n")
                .bitcast(I32),
            )

        def load_plane(g, r):
            nc.sync.dma_start(out=planes[g][r:P:32, :].bitcast(I32), in_=w_attn_scales[g, r:16:4, :].bitcast(I32))

        def load_x_scales():
            for q in range(4):
                nc.sync.dma_start(
                    out=xs[32 * q : 32 * q + 4, :, :].bitcast(I32),
                    in_=x_scales[:, 4 * q : 4 * q + 4, :].rearrange("g r n -> r g n").bitcast(I32),
                )

        nc.sync.dma_start(out=xw[:].bitcast(I32), in_=x_words.rearrange("g p n -> p g n").bitcast(I32))
        load_codes(code_loads[0])
        for r in range(4):
            for g in range(PASSES):
                load_plane(g, r)
                if r == 0 and g == 1:
                    load_codes(code_loads[1])
            if r == 0:
                load_x_scales()
        for item in code_loads[2:]:
            load_codes(item)

        def store(queue, out, a, b, src, h_lo):
            queue.dma_start(
                out=out[0, a:b].rearrange("h p d -> p h d"),
                in_=src[:, h_lo * HEAD : (h_lo + b - a) * HEAD].rearrange("p (h d) -> p h d", d=HEAD),
            )

        for c, (nt, groups) in enumerate(CHUNKS):
            accs = []
            for j in range(nt):
                accs.append(
                    psum.tile([P, TILE], F32, name="acc%d_%d" % (c, j), tag="bank%d" % ((4 * c + j) % BANKS))
                )
            for gi, grp in enumerate(groups):
                t = code_tiles[(c, gi)]
                for k, g in enumerate(grp):
                    for j in range(nt):
                        nc.tensor.matmul_mx(
                            out=accs[j][:],
                            lhsT=xw[:, g, :].bitcast(FP4X4),
                            lhsT_scale=xs[:, g, :],
                            rhs=t[:, k, 2 * j * TILE : 2 * (j + 1) * TILE].bitcast(FP4X4),
                            rhs_scale=planes[g][:, c * CHUNK + j * TILE : c * CHUNK + (j + 1) * TILE],
                            start=(g == 0),
                            stop=(g == PASSES - 1),
                        )

            col0 = c * CHUNK
            col1 = col0 + nt * TILE
            if col0 < ROPE_COLS:
                for j in range(nt):
                    off = col0 + j * TILE
                    toff = off % HEAD
                    nc.vector.tensor_tensor(
                        out=t1[:, off : off + TILE], in0=accs[j][:], in1=cos2[:, toff : toff + TILE], op=MULT
                    )
                    nc.vector.tensor_tensor(
                        out=u[:, off : off + TILE], in0=accs[j][:], in1=sin2[:, toff : toff + TILE], op=MULT
                    )
                h_lo = col0 // HEAD
                h_hi = col1 // HEAD
                rv = t1[:, h_lo * HEAD : h_hi * HEAD].rearrange("p (h s d) -> p h s d", s=2, d=HALF)
                uv = u[:, h_lo * HEAD : h_hi * HEAD].rearrange("p (h s d) -> p h s d", s=2, d=HALF)
                nc.vector.tensor_tensor(out=rv[:, :, 0, :], in0=rv[:, :, 0, :], in1=uv[:, :, 1, :], op=SUB)
                nc.vector.tensor_tensor(out=rv[:, :, 1, :], in0=rv[:, :, 1, :], in1=uv[:, :, 0, :], op=ADD)
                if h_lo < 8:
                    store(nc.gpsimd, out_0, h_lo, min(h_hi, 8), t1, h_lo)
                if h_hi > 8:
                    store(nc.sync if col1 == ROPE_COLS else nc.gpsimd, out_1, max(h_lo, 8) - 8, h_hi - 8, t1, max(h_lo, 8))
            else:
                for j in range(nt):
                    off = col0 - ROPE_COLS + j * TILE
                    if j % 2 == 1:
                        nc.vector.tensor_copy(out=vo[:, off : off + TILE], in_=accs[j][:])
                    else:
                        nc.scalar.copy(out=vo[:, off : off + TILE], in_=accs[j][:])
                h_lo = (col0 - ROPE_COLS) // HEAD
                h_hi = (col1 - ROPE_COLS) // HEAD
                store(nc.sync, out_2, h_lo, h_hi, vo, h_lo)
